import numpy as np
import ml_dtypes


def mxq(x, axis, fmt="e4m3"):
    dtype, down = {"e4m3": (ml_dtypes.float8_e4m3fn, 7), "e5m2": (ml_dtypes.float8_e5m2, 14)}[fmt]
    v = np.moveaxis(np.asarray(x, np.float32).astype(ml_dtypes.bfloat16).astype(np.float64), axis, -1)
    blocks = v.reshape(v.shape[:-1] + (-1, 32))
    amax = np.abs(blocks).max(-1, keepdims=True)
    byte = np.maximum(np.where(amax > 0, np.frexp(amax)[1] - 1 + 127, 0) - down, 1)
    scale = np.exp2(byte - 127.0)
    codes = (blocks / scale).astype(np.float32).astype(dtype).astype(np.float64)
    return np.moveaxis((codes * scale).reshape(v.shape), -1, axis)


WIDE = False


def mx_kscale(k):
    if not WIDE:
        return np.ones(k)
    levels = np.array([30, -30])
    if k % 512:
        return np.exp2(np.random.permutation(np.resize(levels, k // 32))).repeat(32)
    a = np.empty((k // 512, 16))
    for p in range(k // 512):
        a[p, :8] = np.random.permutation(np.resize(levels, 8))
        for g in range(8):
            far = levels[np.abs(levels - a[p, g]) >= 10]
            a[p, g + 8] = far[np.random.randint(len(far))]
    return np.exp2(a.ravel()).repeat(32)


BF16 = ml_dtypes.bfloat16


def bf(x):
    return np.asarray(x, np.float32).astype(BF16)


def f64(x):
    return np.asarray(x).astype(np.float64)


B, D, S, A, H, G = 256, 4096, 1024, 128, 512, 8
DG = D // G


def silu(v):
    return v / (1.0 + np.exp(-v))


def sigmoid(v):
    return 1.0 / (1.0 + np.exp(-v))


def setup_inputs():
    n = np.random.standard_normal
    t = mx_kscale(D)
    return {"y_dyn": bf(silu(n((B, D))) * t), "deter": bf(n((B, D))),
            "gru_W": bf(n((G, DG, 3 * DG)) * 2.0 / np.sqrt(DG) / t.reshape(G, DG)[:, :, None]), "gru_b": bf(n(3 * D) * 0.2)}


def reference(y_dyn, deter, gru_W, gru_b):
    yg = f64(y_dyn).reshape(B, G, DG).transpose(1, 0, 2)
    z = mxq(yg, 2, "e5m2") @ mxq(f64(gru_W), 1, "e4m3")
    z = z.transpose(1, 0, 2).reshape(B, 3 * D) + f64(gru_b)
    reset, cand, update = z[:, :D], z[:, D:2 * D], z[:, 2 * D:]
    reset = sigmoid(reset)
    cand = np.tanh(reset * cand)
    update = sigmoid(update - 1.0)
    return update * cand + (1.0 - update) * f64(deter)

@@ -1,0 +1,281 @@
+from contextlib import ExitStack
+
+import concourse.mybir as mybir
+from concourse.masks import make_identity
+
+F32 = mybir.dt.float32
+BF16 = mybir.dt.bfloat16
+U32 = mybir.dt.uint32
+U8 = mybir.dt.uint8
+E4 = mybir.dt.float8_e4m3fn_x4
+E5 = mybir.dt.float8_e5m2_x4
+ACT = mybir.ActivationFunctionType
+ALU = mybir.AluOpType
+
+FLOPS = 2 * 256 * 512 * 1536 * 8
+
+P = 128
+NH = 16
+R, C, U = 0, 1, 2
+UNIT = {R: 0, U: 256, C: 512}
+SHARES = ((2, (160, 160, 160)), (6, (128, 256, 128)), (99, (0, 256, 0)),)
+
+
+def tile_blockgrucell_pb_kernel(tc, y_dyn, deter, gru_W, gru_b, out):
+    nc = tc.nc
+    y_v = y_dyn.rearrange("(bt p) d -> p bt d", p=P)
+    det_v = deter.rearrange("(bt p) d -> p bt d", p=P)
+    out_v = out.rearrange("(bt p) d -> p bt d", p=P)
+
+    with ExitStack() as ctx:
+        const = ctx.enter_context(tc.tile_pool(name="const", bufs=1))
+        rawp = ctx.enter_context(tc.tile_pool(name="rawp", bufs=1))
+        stgp = ctx.enter_context(tc.tile_pool(name="stgp", bufs=3))
+        cdp = ctx.enter_context(tc.tile_pool(name="cdp", bufs=3))
+        ygp = ctx.enter_context(tc.tile_pool(name="ygp", bufs=2))
+        epp = ctx.enter_context(tc.tile_pool(name="epp", bufs=4))
+        psum = ctx.enter_context(tc.psum_pool(name="psum", bufs=1))
+        ctx.enter_context(tc.manual_schedule())
+
+        ident_f = const.tile([P, P], F32, name="ident_f")
+        ident_b = const.tile([P, P], BF16, name="ident_b")
+        brow = const.tile([P, P], BF16, name="brow")
+        bias = const.tile([P, P], F32, name="bias")
+        warm = const.tile([P, 2], F32, name="warm")
+        ycod = const.tile([P, 2048], U32, name="ycod", align_bytes=64)
+        yscl = const.tile([P, 2048], U8, name="yscl", align_bytes=64)
+
+        y_sb = {}
+        det = {}
+        raw = {}
+        stg = {}
+        cod = {}
+        scl = {}
+        zt = {}
+        at = {}
+        bt_ = {}
+        dts = {}
+        ets = {}
+        ygr = {}
+        xts = {}
+
+        def load_w(q):
+            t = rawp.tile([P, 4, 512], BF16, name="w%d" % q)
+            c0 = 512 * (q % 3)
+            nc.sync.dma_start(out=t[:], in_=gru_W[q // 3, :, c0 : c0 + 512].rearrange("(p j) n -> p j n", j=4))
+            raw[q] = t
+
+        def load_chunk(j):
+            load_w(j)
+            load_w(16 + j)
+            load_w(8 + j)
+
+        def load_y(pr):
+            y_sb[pr] = const.tile([P, 2, 1024], BF16, name="y%d" % pr)
+            nc.sync.dma_start(out=y_sb[pr][:], in_=y_v[:, :, 1024 * pr : 1024 * pr + 1024])
+
+        def load_det(k):
+            det[k] = const.tile([P, 2, 1024], BF16, name="det%d" % k)
+            nc.sync.dma_start(out=det[k][:], in_=det_v[:, :, 1024 * k : 1024 * k + 1024])
+
+        def il(h, gate):
+            if h not in stg:
+                stg[h] = stgp.tile([P, 768, 4], BF16, name="stg", align_bytes=64)
+            nv = [sh for lim, sh in SHARES if h < lim][0][gate]
+            c0 = 256 * (h % 2)
+            u0 = UNIT[gate]
+            w = raw[8 * gate + h // 2]
+            if nv > 0:
+                nc.vector.tensor_copy(out=stg[h][:, u0 : u0 + nv, :], in_=w[:, :, c0 : c0 + nv].rearrange("p j w -> p w j"))
+            if nv < 256:
+                nc.scalar.copy(out=stg[h][:, u0 + nv : u0 + 256, :], in_=w[:, :, c0 + nv : c0 + 256].rearrange("p j w -> p w j"))
+
+        def quantize(h):
+            cod[h] = cdp.tile([P, 768], U32, name="cod", align_bytes=64)
+            scl[h] = cdp.tile([P, 768], U8, name="scl", align_bytes=64)
+            for a, b in ((0, 512), (512, 768)):
+                nc.vector.quantize_mx(
+                    out=cod[h][:, a:b].bitcast(E4),
+                    scales=scl[h][:, a:b],
+                    in_=stg[h][:, a:b, :].rearrange("p w j -> p (w j)"),
+                )
+
+        def mx(h, tau, gate, tag):
+            g = (8 * gate + h // 2) // 3
+            pr = g // 2
+            b0 = UNIT[gate] + P * tau
+            z = psum.tile([P, 512], F32, name=tag, tag=tag, bufs=2)
+            nc.tensor.matmul_mx(
+                out=z[:],
+                lhsT=cod[h][:, b0 : b0 + P].bitcast(E4),
+                lhsT_scale=scl[h][:, b0 : b0 + P],
+                rhs=ycod[:, 512 * pr : 512 * pr + 512].bitcast(E5),
+                rhs_scale=yscl[:, 512 * pr : 512 * pr + 512],
+                start=True,
+                stop=True,
+            )
+            zt[(h, tau, gate)] = z[:, 256 * (g % 2) : 256 * (g % 2) + 256]
+
+        def mx_ru(h):
+            mx(h, 0, R, "zr")
+            mx(h, 1, R, "zr")
+            mx(h, 0, U, "zu")
+            mx(h, 1, U, "zu")
+
+        def mx_c(h):
+            mx(h, 0, C, "zc")
+            mx(h, 1, C, "zc")
+
+        def bcol(h, tau, gate):
+            j = 32 * gate + 2 * h + tau
+            return bias[:, j : j + 1]
+
+        def s1(h):
+            at[h] = epp.tile([P, 512], F32, name="a_t")
+            bt_[h] = epp.tile([P, 512], F32, name="b_t")
+            for tau in (0, 1):
+                nc.scalar.activation(out=at[h][:, 256 * tau : 256 * tau + 256], in_=zt[(h, tau, R)], func=ACT.Sigmoid, bias=bcol(h, tau, R), scale=1.0)
+            for tau in (0, 1):
+                nc.scalar.activation(out=bt_[h][:, 256 * tau : 256 * tau + 256], in_=zt[(h, tau, U)], func=ACT.Sigmoid, bias=bcol(h, tau, U), scale=1.0)
+
+        def v1(h):
+            for tau in (0, 1):
+                sl = at[h][:, 256 * tau : 256 * tau + 256]
+                nc.vector.scalar_tensor_tensor(out=sl, in0=zt[(h, tau, C)], scalar=bcol(h, tau, C), in1=sl, op0=ALU.add, op1=ALU.mult)
+
+        def s2(h):
+            nc.scalar.activation(out=at[h][:], in_=at[h][:], func=ACT.Tanh)
+
+        def p2(h):
+            dts[h] = psum.tile([P, 2, 256], BF16, name="dT", tag="dT", bufs=1)
+            for tau in (0, 1):
+                for b in (0, 1):
+                    n0 = P * (2 * (h % 4) + tau)
+                    nc.tensor.transpose(dts[h][:, tau, P * b : P * b + P], det[h // 4][:, b, n0 : n0 + P], ident_b[:])
+
+        def v2(h):
+            nc.vector.tensor_tensor(out=at[h][:], in0=at[h][:], in1=dts[h][:].rearrange("p t b -> p (t b)"), op=ALU.subtract)
+
+        def v3(h):
+            nc.vector.tensor_tensor(out=at[h][:], in0=at[h][:], in1=bt_[h][:], op=ALU.mult)
+
+        def p3(h):
+            ets[h] = psum.tile([P, 2, 256], F32, name="eT", tag="eT", bufs=1)
+            for tau in (0, 1):
+                for b in (0, 1):
+                    c0 = 256 * tau + P * b
+                    nc.tensor.transpose(ets[h][:, b, P * tau : P * tau + P], at[h][:, c0 : c0 + P], ident_f[:])
+
+        def v4(h):
+            o = epp.tile([P, 2, 256], F32, name="o_t")
+            nc.vector.tensor_tensor(out=o[:], in0=ets[h][:], in1=det[h // 4][:, :, 256 * (h % 4) : 256 * (h % 4) + 256], op=ALU.add)
+            nc.sync.dma_start(out=out_v[:, :, 256 * h : 256 * h + 256], in_=o[:])
+
+        def y_turn(pr, tag):
+            for k in (0, 1):
+                xt = psum.tile([P, 2, 256], F32, name=tag, tag=tag, bufs=2)
+                xts[(pr, k)] = xt
+                for b in (0, 1):
+                    words = y_sb[pr][:, b, :].bitcast(F32)
+                    for u in (0, 1):
+                        nc.tensor.transpose(xt[:, u, P * b : P * b + P], words[:, 256 * k + u : 256 * (k + 1) : 2], ident_f[:])
+
+        def y_copy(pr, engines):
+            ygr[pr] = ygp.tile([P, 512, 4], BF16, name="ygr", align_bytes=64)
+            for k in (0, 1):
+                dst = ygr[pr][:, 256 * k : 256 * k + 256, :].bitcast(F32)
+                if engines[k] == "v":
+                    nc.vector.tensor_copy(out=dst, in_=xts[(pr, k)][:].rearrange("p u b -> p b u"))
+                else:
+                    nc.scalar.copy(out=dst, in_=xts[(pr, k)][:].rearrange("p u b -> p b u"))
+
+        def yquant(pr):
+            nc.vector.quantize_mx(
+                out=ycod[:, 512 * pr : 512 * pr + 512].bitcast(E5),
+                scales=yscl[:, 512 * pr : 512 * pr + 512],
+                in_=ygr[pr][:].rearrange("p w j -> p (w j)"),
+            )
+
+        load_w(0)
+        load_y(0)
+        load_w(16)
+        load_y(2)
+        load_w(8)
+        load_y(1)
+        nc.vector.memset(brow[:], 0.0)
+        nc.vector.memset(warm[:], 0.0)
+        nc.sync.dma_start(out=brow[0:96, :], in_=gru_b.rearrange("(j p) -> j p", p=P))
+        load_chunk(1)
+        load_det(0)
+        load_y(3)
+        load_chunk(2)
+        load_chunk(3)
+        load_det(1)
+        make_identity(nc, ident_f[:])
+        make_identity(nc, ident_b[:])
+        nc.scalar.activation(out=warm[:, 1:2], in_=warm[:, 0:1], func=ACT.Sigmoid)
+
+        il(0, R)
+        il(1, R)
+        y_turn(0, "zr")
+        y_copy(0, "ss")
+        il(0, U)
+        il(1, U)
+        y_turn(2, "zu")
+        y_copy(2, "ss")
+        yquant(0)
+        il(0, C)
+        il(1, C)
+        yquant(2)
+        y_turn(1, "zc")
+        quantize(0)
+        y_copy(1, "ss")
+        bT = psum.tile([P, P], BF16, name="dT", tag="dT", bufs=1)
+        nc.tensor.transpose(bT[:], brow[:], ident_b[:])
+        mx_ru(0)
+        nc.vector.tensor_copy(out=bias[:], in_=bT[:])
+        nc.vector.tensor_scalar_add(out=bias[:, 64:96], in0=bias[:, 64:96], scalar1=-1.0)
+        quantize(1)
+        yquant(1)
+
+        later = {0: (4,), 2: (5,), 4: (6,), 6: (7,)}
+        for t in range(-1, NH + 3):
+            for j in later.get(t, ()):
+                load_chunk(j)
+            if t == 2:
+                load_det(2)
+                load_det(3)
+            if 0 <= t + 1 < NH:
+                s1(t + 1)
+            if 0 <= t < NH:
+                v1(t)
+            if 0 <= t - 2 < NH:
+                p3(t - 2)
+            if t == 1:
+                y_turn(3, "zc")
+            if 0 <= t + 1 < NH and t != 1:
+                mx_c(t + 1)
+            if 2 <= t + 2 < NH:
+                quantize(t + 2)
+            if 1 <= t + 2 < NH:
+                mx_ru(t + 2)
+            if 2 <= t + 3 < NH:
+                il(t + 3, R)
+            if 0 <= t < NH:
+                s2(t)
+            if t == 1:
+                y_copy(3, "vs")
+                mx_c(t + 1)
+            if 0 <= t - 2 < NH:
+                v4(t - 2)
+            if 0 <= t - 1 < NH:
+                v2(t - 1)
+            if 0 <= t < NH:
+                p2(t)
+            if 2 <= t + 3 < NH:
+                il(t + 3, U)
+                il(t + 3, C)
+            if t == 1:
+                yquant(3)
+            if 0 <= t - 1 < NH:
+                v3(t - 1)

@@ -18,7 +18,7 @@ P = 128
 NH = 16
 R, C, U = 0, 1, 2
 UNIT = {R: 0, U: 256, C: 512}
-SHARES = ((2, (160, 160, 160)), (6, (128, 256, 128)), (99, (0, 256, 0)),)
+SHARES = ((2, (160, 160, 160)), (4, (192, 256, 192)), (99, (0, 256, 64)),)
 
 
 def tile_blockgrucell_pb_kernel(tc, y_dyn, deter, gru_W, gru_b, out):
@@ -266,12 +266,12 @@ def tile_blockgrucell_pb_kernel(tc, y_dyn, deter, gru_W, gru_b, out):
             if t == 1:
                 y_copy(3, "vs")
                 mx_c(t + 1)
-            if 0 <= t - 2 < NH:
-                v4(t - 2)
             if 0 <= t - 1 < NH:
                 v2(t - 1)
             if 0 <= t < NH:
                 p2(t)
+            if 0 <= t - 2 < NH:
+                v4(t - 2)
             if 2 <= t + 3 < NH:
                 il(t + 3, U)
                 il(t + 3, C)

@@ -86,9 +86,9 @@ def tile_blockgrucell_pb_kernel(tc, y_dyn, deter, gru_W, gru_b, out):
             u0 = UNIT[gate]
             w = raw[8 * gate + h // 2]
             if nv > 0:
-                nc.vector.tensor_copy(out=stg[h][:, u0 : u0 + nv, :], in_=w[:, :, c0 : c0 + nv].rearrange("p j w -> p w j"))
+                nc.vector.tensor_copy(out=stg[h][:, u0 : u0 + nv, :].rearrange("p (c i) j -> p c j i", i=4), in_=w[:, :, c0 : c0 + nv].rearrange("p j (c i) -> p c j i", i=4))
             if nv < 256:
-                nc.scalar.copy(out=stg[h][:, u0 + nv : u0 + 256, :], in_=w[:, :, c0 + nv : c0 + 256].rearrange("p j w -> p w j"))
+                nc.scalar.copy(out=stg[h][:, u0 + nv : u0 + 256, :].rearrange("p (c i) j -> p c j i", i=4), in_=w[:, :, c0 + nv : c0 + 256].rearrange("p j (c i) -> p c j i", i=4))
 
         def quantize(h):
             cod[h] = cdp.tile([P, 768], U32, name="cod", align_bytes=64)

@@ -18,7 +18,7 @@ P = 128
 NH = 16
 R, C, U = 0, 1, 2
 UNIT = {R: 0, U: 256, C: 512}
-SHARES = ((2, (160, 160, 160)), (4, (192, 256, 192)), (99, (0, 256, 64)),)
+SHARES = ((2, ((160, 0), (160, 0), (160, 0))), (4, ((192, 0), (256, 0), (192, 0))), (99, ((0, 96), (256, 0), (0, 0))),)
 
 
 def tile_blockgrucell_pb_kernel(tc, y_dyn, deter, gru_W, gru_b, out):
@@ -81,14 +81,16 @@ def tile_blockgrucell_pb_kernel(tc, y_dyn, deter, gru_W, gru_b, out):
         def il(h, gate):
             if h not in stg:
                 stg[h] = stgp.tile([P, 768, 4], BF16, name="stg", align_bytes=64)
-            nv = [sh for lim, sh in SHARES if h < lim][0][gate]
+            nv, ng = [sh for lim, sh in SHARES if h < lim][0][gate]
             c0 = 256 * (h % 2)
             u0 = UNIT[gate]
             w = raw[8 * gate + h // 2]
             if nv > 0:
                 nc.vector.tensor_copy(out=stg[h][:, u0 : u0 + nv, :].rearrange("p (c i) j -> p c j i", i=4), in_=w[:, :, c0 : c0 + nv].rearrange("p j (c i) -> p c j i", i=4))
-            if nv < 256:
-                nc.scalar.copy(out=stg[h][:, u0 + nv : u0 + 256, :].rearrange("p (c i) j -> p c j i", i=4), in_=w[:, :, c0 + nv : c0 + 256].rearrange("p j (c i) -> p c j i", i=4))
+            if ng > 0:
+                nc.gpsimd.tensor_scalar(out=stg[h][:, u0 + nv : u0 + nv + ng, :], in0=w[:, :, c0 + nv : c0 + nv + ng].rearrange("p j w -> p w j"), scalar1=1.0, scalar2=0.0, op0=ALU.mult, op1=ALU.add)
+            if nv + ng < 256:
+                nc.scalar.copy(out=stg[h][:, u0 + nv + ng : u0 + 256, :].rearrange("p (c i) j -> p c j i", i=4), in_=w[:, :, c0 + nv + ng : c0 + 256].rearrange("p j (c i) -> p c j i", i=4))
 
         def quantize(h):
             cod[h] = cdp.tile([P, 768], U32, name="cod", align_bytes=64)

@@ -86,11 +86,11 @@ def tile_blockgrucell_pb_kernel(tc, y_dyn, deter, gru_W, gru_b, out):
             u0 = UNIT[gate]
             w = raw[8 * gate + h // 2]
             if nv > 0:
-                nc.vector.tensor_copy(out=stg[h][:, u0 : u0 + nv, :].rearrange("p (c i) j -> p c j i", i=4), in_=w[:, :, c0 : c0 + nv].rearrange("p j (c i) -> p c j i", i=4))
+                nc.vector.tensor_copy(out=stg[h][:, u0 : u0 + nv, :].rearrange("p (c i) j -> p c j i", i=8), in_=w[:, :, c0 : c0 + nv].rearrange("p j (c i) -> p c j i", i=8))
             if ng > 0:
                 nc.gpsimd.tensor_scalar(out=stg[h][:, u0 + nv : u0 + nv + ng, :], in0=w[:, :, c0 + nv : c0 + nv + ng].rearrange("p j w -> p w j"), scalar1=1.0, scalar2=0.0, op0=ALU.mult, op1=ALU.add)
             if nv + ng < 256:
-                nc.scalar.copy(out=stg[h][:, u0 + nv + ng : u0 + 256, :].rearrange("p (c i) j -> p c j i", i=4), in_=w[:, :, c0 + nv + ng : c0 + 256].rearrange("p j (c i) -> p c j i", i=4))
+                nc.scalar.copy(out=stg[h][:, u0 + nv + ng : u0 + 256, :].rearrange("p (c i) j -> p c j i", i=8), in_=w[:, :, c0 + nv + ng : c0 + 256].rearrange("p j (c i) -> p c j i", i=8))
 
         def quantize(h):
             cod[h] = cdp.tile([P, 768], U32, name="cod", align_bytes=64)

@@ -18,7 +18,7 @@ P = 128
 NH = 16
 R, C, U = 0, 1, 2
 UNIT = {R: 0, U: 256, C: 512}
-SHARES = ((2, ((160, 0), (160, 0), (160, 0))), (4, ((192, 0), (256, 0), (192, 0))), (99, ((0, 96), (256, 0), (0, 0))),)
+SHARES = ((2, ((160, 0), (160, 0), (160, 0))), (4, ((192, 0), (256, 0), (192, 0))), (99, ((160, 96), (256, 0), (0, 0))),)
 
 
 def tile_blockgrucell_pb_kernel(tc, y_dyn, deter, gru_W, gru_b, out):
@@ -163,14 +163,16 @@ def tile_blockgrucell_pb_kernel(tc, y_dyn, deter, gru_W, gru_b, out):
 
         def p3(h):
             ets[h] = psum.tile([P, 2, 256], F32, name="eT", tag="eT", bufs=1)
+            n0 = 256 * (h % 4)
+            nc.tensor.matmul(out=ets[h][:], lhsT=ident_b[:], rhs=det[h // 4][:, :, n0 : n0 + 256], start=True, stop=False)
             for tau in (0, 1):
                 for b in (0, 1):
                     c0 = 256 * tau + P * b
-                    nc.tensor.transpose(ets[h][:, b, P * tau : P * tau + P], at[h][:, c0 : c0 + P], ident_f[:])
+                    nc.tensor.matmul(out=ets[h][:, b, P * tau : P * tau + P], lhsT=at[h][:, c0 : c0 + P], rhs=ident_f[:], is_transpose=True, start=False, stop=(tau == 1 and b == 1))
 
         def v4(h):
             o = epp.tile([P, 2, 256], F32, name="o_t")
-            nc.vector.tensor_tensor(out=o[:], in0=ets[h][:], in1=det[h // 4][:, :, 256 * (h % 4) : 256 * (h % 4) + 256], op=ALU.add)
+            nc.scalar.copy(out=o[:], in_=ets[h][:])
             nc.sync.dma_start(out=out_v[:, :, 256 * h : 256 * h + 256], in_=o[:])
 
         def y_turn(pr, tag):

@@ -17,6 +17,7 @@ FLOPS = 2 * 256 * 512 * 1536 * 8
 P = 128
 NH = 16
 R, C, U = 0, 1, 2
+YORD = (0, 5, 2, 3, 6, 1, 4, 7)
 UNIT = {R: 0, U: 256, C: 512}
 SHARES = ((2, ((160, 0), (160, 0), (160, 0))), (4, ((192, 0), (256, 0), (192, 0))), (99, ((160, 96), (256, 0), (0, 0))),)
 
@@ -32,7 +33,7 @@ def tile_blockgrucell_pb_kernel(tc, y_dyn, deter, gru_W, gru_b, out):
         rawp = ctx.enter_context(tc.tile_pool(name="rawp", bufs=1))
         stgp = ctx.enter_context(tc.tile_pool(name="stgp", bufs=3))
         cdp = ctx.enter_context(tc.tile_pool(name="cdp", bufs=3))
-        ygp = ctx.enter_context(tc.tile_pool(name="ygp", bufs=2))
+        ygp = ctx.enter_context(tc.tile_pool(name="ygp", bufs=3))
         epp = ctx.enter_context(tc.tile_pool(name="epp", bufs=4))
         psum = ctx.enter_context(tc.psum_pool(name="psum", bufs=1))
         ctx.enter_context(tc.manual_schedule())
@@ -70,9 +71,9 @@ def tile_blockgrucell_pb_kernel(tc, y_dyn, deter, gru_W, gru_b, out):
             load_w(16 + j)
             load_w(8 + j)
 
-        def load_y(pr):
-            y_sb[pr] = const.tile([P, 2, 1024], BF16, name="y%d" % pr)
-            nc.sync.dma_start(out=y_sb[pr][:], in_=y_v[:, :, 1024 * pr : 1024 * pr + 1024])
+        def load_y(g):
+            y_sb[g] = const.tile([P, 2, 512], BF16, name="y%d" % g)
+            nc.sync.dma_start(out=y_sb[g][:], in_=y_v[:, :, 512 * g : 512 * g + 512])
 
         def load_det(k):
             det[k] = const.tile([P, 2, 1024], BF16, name="det%d" % k)
@@ -92,10 +93,11 @@ def tile_blockgrucell_pb_kernel(tc, y_dyn, deter, gru_W, gru_b, out):
             if nv + ng < 256:
                 nc.scalar.copy(out=stg[h][:, u0 + nv + ng : u0 + 256, :].rearrange("p (c i) j -> p c j i", i=8), in_=w[:, :, c0 + nv + ng : c0 + 256].rearrange("p j (c i) -> p c j i", i=8))
 
-        def quantize(h):
-            cod[h] = cdp.tile([P, 768], U32, name="cod", align_bytes=64)
-            scl[h] = cdp.tile([P, 768], U8, name="scl", align_bytes=64)
-            for a, b in ((0, 512), (512, 768)):
+        def quantize(h, parts=((0, 512), (512, 768))):
+            if h not in cod:
+                cod[h] = cdp.tile([P, 768], U32, name="cod", align_bytes=64)
+                scl[h] = cdp.tile([P, 768], U8, name="scl", align_bytes=64)
+            for a, b in parts:
                 nc.vector.quantize_mx(
                     out=cod[h][:, a:b].bitcast(E4),
                     scales=scl[h][:, a:b],
@@ -104,19 +106,21 @@ def tile_blockgrucell_pb_kernel(tc, y_dyn, deter, gru_W, gru_b, out):
 
         def mx(h, tau, gate, tag):
             g = (8 * gate + h // 2) // 3
-            pr = g // 2
+            pos = YORD.index(g)
+            y0 = 256 * max(pos - 1, 0)
+            half = 256 * pos - y0
             b0 = UNIT[gate] + P * tau
             z = psum.tile([P, 512], F32, name=tag, tag=tag, bufs=2)
             nc.tensor.matmul_mx(
                 out=z[:],
                 lhsT=cod[h][:, b0 : b0 + P].bitcast(E4),
                 lhsT_scale=scl[h][:, b0 : b0 + P],
-                rhs=ycod[:, 512 * pr : 512 * pr + 512].bitcast(E5),
-                rhs_scale=yscl[:, 512 * pr : 512 * pr + 512],
+                rhs=ycod[:, y0 : y0 + 512].bitcast(E5),
+                rhs_scale=yscl[:, y0 : y0 + 512],
                 start=True,
                 stop=True,
             )
-            zt[(h, tau, gate)] = z[:, 256 * (g % 2) : 256 * (g % 2) + 256]
+            zt[(h, tau, gate)] = z[:, half : half + 256]
 
         def mx_ru(h):
             mx(h, 0, R, "zr")
@@ -145,8 +149,12 @@ def tile_blockgrucell_pb_kernel(tc, y_dyn, deter, gru_W, gru_b, out):
                 sl = at[h][:, 256 * tau : 256 * tau + 256]
                 nc.vector.scalar_tensor_tensor(out=sl, in0=zt[(h, tau, C)], scalar=bcol(h, tau, C), in1=sl, op0=ALU.add, op1=ALU.mult)
 
+        def pieces(h):
+            return ((0, 256), (256, 512)) if h == NH - 1 else ((0, 512),)
+
         def s2(h):
-            nc.scalar.activation(out=at[h][:], in_=at[h][:], func=ACT.Tanh)
+            for a, b in pieces(h):
+                nc.scalar.activation(out=at[h][:, a:b], in_=at[h][:, a:b], func=ACT.Tanh)
 
         def p2(h):
             dts[h] = psum.tile([P, 2, 256], BF16, name="dT", tag="dT", bufs=1)
@@ -156,63 +164,70 @@ def tile_blockgrucell_pb_kernel(tc, y_dyn, deter, gru_W, gru_b, out):
                     nc.tensor.transpose(dts[h][:, tau, P * b : P * b + P], det[h // 4][:, b, n0 : n0 + P], ident_b[:])
 
         def v2(h):
-            nc.vector.tensor_tensor(out=at[h][:], in0=at[h][:], in1=dts[h][:].rearrange("p t b -> p (t b)"), op=ALU.subtract)
+            for a, b in pieces(h):
+                nc.vector.tensor_tensor(out=at[h][:, a:b], in0=at[h][:, a:b], in1=dts[h][:].rearrange("p t b -> p (t b)")[:, a:b], op=ALU.subtract)
 
         def v3(h):
-            nc.vector.tensor_tensor(out=at[h][:], in0=at[h][:], in1=bt_[h][:], op=ALU.mult)
+            for a, b in pieces(h):
+                nc.vector.tensor_tensor(out=at[h][:, a:b], in0=at[h][:, a:b], in1=bt_[h][:, a:b], op=ALU.mult)
 
         def p3(h):
-            ets[h] = psum.tile([P, 2, 256], F32, name="eT", tag="eT", bufs=1)
-            n0 = 256 * (h % 4)
-            nc.tensor.matmul(out=ets[h][:], lhsT=ident_b[:], rhs=det[h // 4][:, :, n0 : n0 + 256], start=True, stop=False)
-            for tau in (0, 1):
-                for b in (0, 1):
-                    c0 = 256 * tau + P * b
-                    nc.tensor.matmul(out=ets[h][:, b, P * tau : P * tau + P], lhsT=at[h][:, c0 : c0 + P], rhs=ident_f[:], is_transpose=True, start=False, stop=(tau == 1 and b == 1))
+            ets[h] = []
+            for i, (a, b) in enumerate(pieces(h)):
+                w = (b - a) // 2
+                n0 = 256 * (h % 4) + a // 2
+                e = psum.tile([P, 2, w], F32, name="eT", tag=("eT", "dT")[i], bufs=1)
+                ets[h].append(e)
+                nc.tensor.matmul(out=e[:], lhsT=ident_b[:], rhs=det[h // 4][:, :, n0 : n0 + w], start=True, stop=False)
+                for s in range(w // P):
+                    for bb in (0, 1):
+                        c0 = a + 256 * s + P * bb
+                        nc.tensor.matmul(out=e[:, bb, P * s : P * s + P], lhsT=at[h][:, c0 : c0 + P], rhs=ident_f[:], is_transpose=True, start=False, stop=(s == w // P - 1 and bb == 1))
 
         def v4(h):
-            o = epp.tile([P, 2, 256], F32, name="o_t")
-            nc.scalar.copy(out=o[:], in_=ets[h][:])
-            nc.sync.dma_start(out=out_v[:, :, 256 * h : 256 * h + 256], in_=o[:])
+            for i, (a, b) in enumerate(pieces(h)):
+                w = (b - a) // 2
+                o = epp.tile([P, 2, w], F32, name="o_t")
+                nc.scalar.copy(out=o[:], in_=ets[h][i][:])
+                nc.sync.dma_start(out=out_v[:, :, 256 * h + a // 2 : 256 * h + a // 2 + w], in_=o[:])
 
-        def y_turn(pr, tag):
-            for k in (0, 1):
-                xt = psum.tile([P, 2, 256], F32, name=tag, tag=tag, bufs=2)
-                xts[(pr, k)] = xt
-                for b in (0, 1):
-                    words = y_sb[pr][:, b, :].bitcast(F32)
-                    for u in (0, 1):
-                        nc.tensor.transpose(xt[:, u, P * b : P * b + P], words[:, 256 * k + u : 256 * (k + 1) : 2], ident_f[:])
+        def y_turn(g, tag, bufs):
+            xt = psum.tile([P, 2, 256], F32, name=tag, tag=tag, bufs=bufs)
+            xts[g] = xt
+            for b in (0, 1):
+                words = y_sb[g][:, b, :].bitcast(F32)
+                for u in (0, 1):
+                    nc.tensor.transpose(xt[:, u, P * b : P * b + P], words[:, u : 256 : 2], ident_f[:])
 
-        def y_copy(pr, engines):
-            ygr[pr] = ygp.tile([P, 512, 4], BF16, name="ygr", align_bytes=64)
-            for k in (0, 1):
-                dst = ygr[pr][:, 256 * k : 256 * k + 256, :].bitcast(F32)
-                if engines[k] == "v":
-                    nc.vector.tensor_copy(out=dst, in_=xts[(pr, k)][:].rearrange("p u b -> p b u"))
-                else:
-                    nc.scalar.copy(out=dst, in_=xts[(pr, k)][:].rearrange("p u b -> p b u"))
+        def y_copy(g):
+            ygr[g] = ygp.tile([P, 256, 4], BF16, name="ygr", align_bytes=64)
+            nc.scalar.copy(out=ygr[g][:].bitcast(F32), in_=xts[g][:].rearrange("p u b -> p b u"))
 
-        def yquant(pr):
+        def yquant(g):
+            c0 = 256 * YORD.index(g)
             nc.vector.quantize_mx(
-                out=ycod[:, 512 * pr : 512 * pr + 512].bitcast(E5),
-                scales=yscl[:, 512 * pr : 512 * pr + 512],
-                in_=ygr[pr][:].rearrange("p w j -> p (w j)"),
+                out=ycod[:, c0 : c0 + 256].bitcast(E5),
+                scales=yscl[:, c0 : c0 + 256],
+                in_=ygr[g][:].rearrange("p w j -> p (w j)"),
             )
 
         load_w(0)
         load_y(0)
         load_w(16)
-        load_y(2)
+        load_y(5)
         load_w(8)
-        load_y(1)
+        load_y(2)
         nc.vector.memset(brow[:], 0.0)
         nc.vector.memset(warm[:], 0.0)
         nc.sync.dma_start(out=brow[0:96, :], in_=gru_b.rearrange("(j p) -> j p", p=P))
         load_chunk(1)
-        load_det(0)
         load_y(3)
+        load_y(6)
+        load_det(0)
+        load_y(1)
+        load_y(4)
         load_chunk(2)
+        load_y(7)
         load_chunk(3)
         load_det(1)
         make_identity(nc, ident_f[:])
@@ -221,27 +236,35 @@ def tile_blockgrucell_pb_kernel(tc, y_dyn, deter, gru_W, gru_b, out):
 
         il(0, R)
         il(1, R)
-        y_turn(0, "zr")
-        y_copy(0, "ss")
+        y_turn(0, "zr", 2)
+        y_copy(0)
         il(0, U)
         il(1, U)
-        y_turn(2, "zu")
-        y_copy(2, "ss")
+        y_turn(5, "zu", 2)
+        y_copy(5)
+        quantize(0, ((0, 512),))
         yquant(0)
+        quantize(1, ((0, 512),))
         il(0, C)
         il(1, C)
-        yquant(2)
-        y_turn(1, "zc")
-        quantize(0)
-        y_copy(1, "ss")
+        yquant(5)
+        y_turn(2, "zc", 2)
+        y_copy(2)
         bT = psum.tile([P, P], BF16, name="dT", tag="dT", bufs=1)
         nc.tensor.transpose(bT[:], brow[:], ident_b[:])
         mx_ru(0)
+        quantize(0, ((512, 768),))
         nc.vector.tensor_copy(out=bias[:], in_=bT[:])
         nc.vector.tensor_scalar_add(out=bias[:, 64:96], in0=bias[:, 64:96], scalar1=-1.0)
-        quantize(1)
-        yquant(1)
+        yquant(2)
+        quantize(1, ((512, 768),))
 
+        turn_a = {1: ((4, "eT"),)}
+        turn_b = {-1: ((3, "eT"), (6, "dT")), 0: ((1, "eT"),), 1: ((7, "eT"),)}
+        copy_a = {1: (4,)}
+        copy_b = {-1: (3, 6), 0: (1,), 1: (7,)}
+        quant_q = {0: (3, 6), 1: (1,), 2: (7,)}
+        quant_e = {1: (4,)}
         later = {0: (4,), 2: (5,), 4: (6,), 6: (7,)}
         for t in range(-1, NH + 3):
             for j in later.get(t, ()):
@@ -249,27 +272,28 @@ def tile_blockgrucell_pb_kernel(tc, y_dyn, deter, gru_W, gru_b, out):
             if t == 2:
                 load_det(2)
                 load_det(3)
+            for g, tag in turn_a.get(t, ()):
+                y_turn(g, tag, 1)
             if 0 <= t + 1 < NH:
                 s1(t + 1)
+            for g in copy_a.get(t, ()):
+                y_copy(g)
             if 0 <= t < NH:
                 v1(t)
             if 0 <= t - 2 < NH:
                 p3(t - 2)
-            if t == 1:
-                y_turn(3, "zc")
-            if 0 <= t + 1 < NH and t != 1:
+            if 0 <= t + 1 < NH:
                 mx_c(t + 1)
             if 2 <= t + 2 < NH:
                 quantize(t + 2)
+            for g in quant_q.get(t, ()):
+                yquant(g)
             if 1 <= t + 2 < NH:
                 mx_ru(t + 2)
             if 2 <= t + 3 < NH:
                 il(t + 3, R)
             if 0 <= t < NH:
                 s2(t)
-            if t == 1:
-                y_copy(3, "vs")
-                mx_c(t + 1)
             if 0 <= t - 1 < NH:
                 v2(t - 1)
             if 0 <= t < NH:
@@ -279,7 +303,11 @@ def tile_blockgrucell_pb_kernel(tc, y_dyn, deter, gru_W, gru_b, out):
             if 2 <= t + 3 < NH:
                 il(t + 3, U)
                 il(t + 3, C)
-            if t == 1:
-                yquant(3)
+            for g, tag in turn_b.get(t, ()):
+                y_turn(g, tag, 1)
+            for g in copy_b.get(t, ()):
+                y_copy(g)
+            for g in quant_e.get(t, ()):
+                yquant(g)
             if 0 <= t - 1 < NH:
                 v3(t - 1)

@@ -187,7 +187,7 @@ def tile_blockgrucell_pb_kernel(tc, y_dyn, deter, gru_W, gru_b, out):
         def v4(h):
             for i, (a, b) in enumerate(pieces(h)):
                 w = (b - a) // 2
-                o = epp.tile([P, 2, w], F32, name="o_t")
+                o = epp.tile([P, 2, w], F32, name="o_t", bufs=8)
                 nc.scalar.copy(out=o[:], in_=ets[h][i][:])
                 nc.sync.dma_start(out=out_v[:, :, 256 * h + a // 2 : 256 * h + a // 2 + w], in_=o[:])
 

@@ -19,7 +19,7 @@ NH = 16
 R, C, U = 0, 1, 2
 YORD = (0, 5, 2, 3, 6, 1, 4, 7)
 UNIT = {R: 0, U: 256, C: 512}
-SHARES = ((2, ((160, 0), (160, 0), (160, 0))), (4, ((192, 0), (256, 0), (192, 0))), (99, ((160, 96), (256, 0), (0, 0))),)
+SHARES = ((2, ((160, 0), (160, 0), (160, 0))), (4, ((192, 0), (256, 0), (192, 0))), (99, ((64, 192), (256, 0), (0, 0))),)
 
 
 def tile_blockgrucell_pb_kernel(tc, y_dyn, deter, gru_W, gru_b, out):
@@ -79,18 +79,18 @@ def tile_blockgrucell_pb_kernel(tc, y_dyn, deter, gru_W, gru_b, out):
             det[k] = const.tile([P, 2, 1024], BF16, name="det%d" % k)
             nc.sync.dma_start(out=det[k][:], in_=det_v[:, :, 1024 * k : 1024 * k + 1024])
 
-        def il(h, gate):
+        def il(h, gate, eng="vgs"):
             if h not in stg:
                 stg[h] = stgp.tile([P, 768, 4], BF16, name="stg", align_bytes=64)
             nv, ng = [sh for lim, sh in SHARES if h < lim][0][gate]
             c0 = 256 * (h % 2)
             u0 = UNIT[gate]
             w = raw[8 * gate + h // 2]
-            if nv > 0:
+            if nv > 0 and "v" in eng:
                 nc.vector.tensor_copy(out=stg[h][:, u0 : u0 + nv, :].rearrange("p (c i) j -> p c j i", i=8), in_=w[:, :, c0 : c0 + nv].rearrange("p j (c i) -> p c j i", i=8))
-            if ng > 0:
+            if ng > 0 and "g" in eng:
                 nc.gpsimd.tensor_scalar(out=stg[h][:, u0 + nv : u0 + nv + ng, :], in0=w[:, :, c0 + nv : c0 + nv + ng].rearrange("p j w -> p w j"), scalar1=1.0, scalar2=0.0, op0=ALU.mult, op1=ALU.add)
-            if nv + ng < 256:
+            if nv + ng < 256 and "s" in eng:
                 nc.scalar.copy(out=stg[h][:, u0 + nv + ng : u0 + 256, :].rearrange("p (c i) j -> p c j i", i=8), in_=w[:, :, c0 + nv + ng : c0 + 256].rearrange("p j (c i) -> p c j i", i=8))
 
         def quantize(h, parts=((0, 512), (512, 768))):
@@ -278,31 +278,32 @@ def tile_blockgrucell_pb_kernel(tc, y_dyn, deter, gru_W, gru_b, out):
                 s1(t + 1)
             for g in copy_a.get(t, ()):
                 y_copy(g)
-            if 0 <= t < NH:
-                v1(t)
             if 0 <= t - 2 < NH:
                 p3(t - 2)
-            if 0 <= t + 1 < NH:
-                mx_c(t + 1)
             if 2 <= t + 2 < NH:
                 quantize(t + 2)
-            for g in quant_q.get(t, ()):
-                yquant(g)
+            if 0 <= t < NH:
+                v1(t)
+            if 0 <= t + 1 < NH:
+                mx_c(t + 1)
             if 1 <= t + 2 < NH:
                 mx_ru(t + 2)
             if 2 <= t + 3 < NH:
-                il(t + 3, R)
-            if 0 <= t < NH:
-                s2(t)
+                il(t + 3, U, "s")
             if 0 <= t - 1 < NH:
                 v2(t - 1)
             if 0 <= t < NH:
                 p2(t)
+            if 0 <= t < NH:
+                s2(t)
+            if 2 <= t + 3 < NH:
+                il(t + 3, R, "vgs")
+                il(t + 3, U, "vg")
+                il(t + 3, C, "vgs")
+            for g in quant_q.get(t, ()):
+                yquant(g)
             if 0 <= t - 2 < NH:
                 v4(t - 2)
-            if 2 <= t + 3 < NH:
-                il(t + 3, U)
-                il(t + 3, C)
             for g, tag in turn_b.get(t, ()):
                 y_turn(g, tag, 1)
             for g in copy_b.get(t, ()):

@@ -19,7 +19,7 @@ NH = 16
 R, C, U = 0, 1, 2
 YORD = (0, 5, 2, 3, 6, 1, 4, 7)
 UNIT = {R: 0, U: 256, C: 512}
-SHARES = ((2, ((160, 0), (160, 0), (160, 0))), (4, ((192, 0), (256, 0), (192, 0))), (99, ((64, 192), (256, 0), (0, 0))),)
+SHARES = ((2, ((160, 0), (160, 0), (160, 0))), (4, ((192, 0), (256, 0), (192, 0))), (5, ((256, 0), (256, 0), (0, 0))), (99, ((256, 0), (80, 176), (0, 0))),)
 
 
 def tile_blockgrucell_pb_kernel(tc, y_dyn, deter, gru_W, gru_b, out):
@@ -80,20 +80,25 @@ def tile_blockgrucell_pb_kernel(tc, y_dyn, deter, gru_W, gru_b, out):
             nc.sync.dma_start(out=det[k][:], in_=det_v[:, :, 1024 * k : 1024 * k + 1024])
 
         def il(h, gate, eng="vgs"):
-            if h not in stg:
-                stg[h] = stgp.tile([P, 768, 4], BF16, name="stg", align_bytes=64)
+            key = (h, gate == C)
+            if key not in stg:
+                if gate == C:
+                    stg[key] = stgp.tile([P, 256, 4], BF16, name="stg_c", align_bytes=64, bufs=2)
+                else:
+                    stg[key] = stgp.tile([P, 512, 4], BF16, name="stg_ru", align_bytes=64)
+            st = stg[key]
             nv, ng = [sh for lim, sh in SHARES if h < lim][0][gate]
             c0 = 256 * (h % 2)
-            u0 = UNIT[gate]
+            u0 = UNIT[gate] % 512
             w = raw[8 * gate + h // 2]
             if nv > 0 and "v" in eng:
-                nc.vector.tensor_copy(out=stg[h][:, u0 : u0 + nv, :].rearrange("p (c i) j -> p c j i", i=8), in_=w[:, :, c0 : c0 + nv].rearrange("p j (c i) -> p c j i", i=8))
+                nc.vector.tensor_copy(out=st[:, u0 : u0 + nv, :].rearrange("p (c i) j -> p c j i", i=8), in_=w[:, :, c0 : c0 + nv].rearrange("p j (c i) -> p c j i", i=8))
             if ng > 0 and "g" in eng:
-                nc.gpsimd.tensor_scalar(out=stg[h][:, u0 + nv : u0 + nv + ng, :], in0=w[:, :, c0 + nv : c0 + nv + ng].rearrange("p j w -> p w j"), scalar1=1.0, scalar2=0.0, op0=ALU.mult, op1=ALU.add)
+                nc.gpsimd.tensor_scalar(out=st[:, u0 + nv : u0 + nv + ng, :], in0=w[:, :, c0 + nv : c0 + nv + ng].rearrange("p j w -> p w j"), scalar1=1.0, scalar2=0.0, op0=ALU.mult, op1=ALU.add)
             if nv + ng < 256 and "s" in eng:
-                nc.scalar.copy(out=stg[h][:, u0 + nv + ng : u0 + 256, :].rearrange("p (c i) j -> p c j i", i=8), in_=w[:, :, c0 + nv + ng : c0 + 256].rearrange("p j (c i) -> p c j i", i=8))
+                nc.scalar.copy(out=st[:, u0 + nv + ng : u0 + 256, :].rearrange("p (c i) j -> p c j i", i=8), in_=w[:, :, c0 + nv + ng : c0 + 256].rearrange("p j (c i) -> p c j i", i=8))
 
-        def quantize(h, parts=((0, 512), (512, 768))):
+        def quantize(h, parts=((512, 768), (0, 512))):
             if h not in cod:
                 cod[h] = cdp.tile([P, 768], U32, name="cod", align_bytes=64)
                 scl[h] = cdp.tile([P, 768], U8, name="scl", align_bytes=64)
@@ -101,7 +106,7 @@ def tile_blockgrucell_pb_kernel(tc, y_dyn, deter, gru_W, gru_b, out):
                 nc.vector.quantize_mx(
                     out=cod[h][:, a:b].bitcast(E4),
                     scales=scl[h][:, a:b],
-                    in_=stg[h][:, a:b, :].rearrange("p w j -> p (w j)"),
+                    in_=stg[(h, a == 512)][:].rearrange("p w j -> p (w j)"),
                 )
 
         def mx(h, tau, gate, tag):

@@ -19,7 +19,7 @@ NH = 16
 R, C, U = 0, 1, 2
 YORD = (0, 5, 2, 3, 6, 1, 4, 7)
 UNIT = {R: 0, U: 256, C: 512}
-SHARES = ((2, ((160, 0), (160, 0), (160, 0))), (4, ((192, 0), (256, 0), (192, 0))), (5, ((256, 0), (256, 0), (0, 0))), (99, ((256, 0), (80, 176), (0, 0))),)
+SHARES = ((2, ((160, 0), (160, 0), (160, 0))), (4, ((192, 0), (256, 0), (192, 0))), (5, ((256, 0), (256, 0), (0, 0))), (99, ((256, 0), (80, 176), (16, 0))),)
 
 
 def tile_blockgrucell_pb_kernel(tc, y_dyn, deter, gru_W, gru_b, out):

@@ -266,8 +266,8 @@ def tile_blockgrucell_pb_kernel(tc, y_dyn, deter, gru_W, gru_b, out):
 
         turn_a = {1: ((4, "eT"),)}
         turn_b = {-1: ((3, "eT"), (6, "dT")), 0: ((1, "eT"),), 1: ((7, "eT"),)}
-        copy_a = {1: (4,)}
-        copy_b = {-1: (3, 6), 0: (1,), 1: (7,)}
+        copy_a = {0: (3, 6), 1: (4,)}
+        copy_b = {0: (1,), 1: (7,)}
         quant_q = {0: (3, 6), 1: (1,), 2: (7,)}
         quant_e = {1: (4,)}
         later = {0: (4,), 2: (5,), 4: (6,), 6: (7,)}
@@ -289,10 +289,14 @@ def tile_blockgrucell_pb_kernel(tc, y_dyn, deter, gru_W, gru_b, out):
                 quantize(t + 2)
             if 0 <= t < NH:
                 v1(t)
-            if 0 <= t + 1 < NH:
+            if t < 2 and 0 <= t + 1 < NH:
                 mx_c(t + 1)
             if 1 <= t + 2 < NH:
                 mx_ru(t + 2)
+            if 2 <= t < NH - 1:
+                mx_c(t + 1)
+            if 0 <= t - 2 < NH:
+                v4(t - 2)
             if 2 <= t + 3 < NH:
                 il(t + 3, U, "s")
             if 0 <= t - 1 < NH:
@@ -307,8 +311,6 @@ def tile_blockgrucell_pb_kernel(tc, y_dyn, deter, gru_W, gru_b, out):
                 il(t + 3, C, "vgs")
             for g in quant_q.get(t, ()):
                 yquant(g)
-            if 0 <= t - 2 < NH:
-                v4(t - 2)
             for g, tag in turn_b.get(t, ()):
                 y_turn(g, tag, 1)
             for g in copy_b.get(t, ()):

@@ -19,7 +19,10 @@ NH = 16
 R, C, U = 0, 1, 2
 YORD = (0, 5, 2, 3, 6, 1, 4, 7)
 UNIT = {R: 0, U: 256, C: 512}
-SHARES = ((2, ((160, 0), (160, 0), (160, 0))), (4, ((192, 0), (256, 0), (192, 0))), (5, ((256, 0), (256, 0), (0, 0))), (99, ((256, 0), (80, 176), (16, 0))),)
+SHARES = ((2, ((160, 0), (160, 0), (160, 0))), (4, ((192, 0), (256, 0), (192, 0))), (5, ((256, 0), (256, 0), (0, 0))), (99, ((256, 0), (80, 176), (0, 0))),)
+
+TAIL_E = {13: (("zr", 2),), 14: (("zu", 2),)}
+TAIL_D = {14: ("zu", 2), 15: ("zu", 2)}
 
 
 def tile_blockgrucell_pb_kernel(tc, y_dyn, deter, gru_W, gru_b, out):
@@ -162,7 +165,8 @@ def tile_blockgrucell_pb_kernel(tc, y_dyn, deter, gru_W, gru_b, out):
                 nc.scalar.activation(out=at[h][:, a:b], in_=at[h][:, a:b], func=ACT.Tanh)
 
         def p2(h):
-            dts[h] = psum.tile([P, 2, 256], BF16, name="dT", tag="dT", bufs=1)
+            tag, bufs = TAIL_D.get(h, ("dT", 1))
+            dts[h] = psum.tile([P, 2, 256], BF16, name="dT", tag=tag, bufs=bufs)
             for tau in (0, 1):
                 for b in (0, 1):
                     n0 = P * (2 * (h % 4) + tau)
@@ -181,7 +185,8 @@ def tile_blockgrucell_pb_kernel(tc, y_dyn, deter, gru_W, gru_b, out):
             for i, (a, b) in enumerate(pieces(h)):
                 w = (b - a) // 2
                 n0 = 256 * (h % 4) + a // 2
-                e = psum.tile([P, 2, w], F32, name="eT", tag=("eT", "dT")[i], bufs=1)
+                tag, bufs = TAIL_E.get(h, (("eT", 1), ("dT", 1)))[i]
+                e = psum.tile([P, 2, w], F32, name="eT", tag=tag, bufs=bufs)
                 ets[h].append(e)
                 nc.tensor.matmul(out=e[:], lhsT=ident_b[:], rhs=det[h // 4][:, :, n0 : n0 + w], start=True, stop=False)
                 for s in range(w // P):
@@ -295,10 +300,10 @@ def tile_blockgrucell_pb_kernel(tc, y_dyn, deter, gru_W, gru_b, out):
                 mx_ru(t + 2)
             if 2 <= t < NH - 1:
                 mx_c(t + 1)
-            if 0 <= t - 2 < NH:
-                v4(t - 2)
             if 2 <= t + 3 < NH:
                 il(t + 3, U, "s")
+            if 0 <= t - 2 < NH:
+                v4(t - 2)
             if 0 <= t - 1 < NH:
                 v2(t - 1)
             if 0 <= t < NH:

@@ -21,8 +21,13 @@ YORD = (0, 5, 2, 3, 6, 1, 4, 7)
 UNIT = {R: 0, U: 256, C: 512}
 SHARES = ((2, ((160, 0), (160, 0), (160, 0))), (4, ((192, 0), (256, 0), (192, 0))), (5, ((256, 0), (256, 0), (0, 0))), (99, ((256, 0), (80, 176), (0, 0))),)
 
-TAIL_E = {13: (("zr", 2),), 14: (("zu", 2),)}
-TAIL_D = {14: ("zu", 2), 15: ("zu", 2)}
+D_BANK = {13: "eT", 14: "zu", 15: "zu"}
+E_BANK = {13: ("zr",), 15: ("eT", "zr")}
+Y_TURN = {-1: (3, 6), 0: (1,), 2: (4,), 4: (7,)}
+Y_COPY = {0: (3, 6), 1: (1,), 3: (4,), 5: (7,)}
+Y_QUANT = {0: (3, 6), 2: (1,), 4: (4,), 6: (7,)}
+HEAD = (("c", 1), ("y", 3), ("y", 6), ("d", 0), ("y", 1), ("c", 2), ("y", 4), ("y", 7), ("c", 3), ("d", 1))
+LATER = {0: (("c", 4),), 2: (("c", 5), ("d", 2), ("d", 3)), 4: (("c", 6),), 6: (("c", 7),)}
 
 
 def tile_blockgrucell_pb_kernel(tc, y_dyn, deter, gru_W, gru_b, out):
@@ -56,6 +61,7 @@ def tile_blockgrucell_pb_kernel(tc, y_dyn, deter, gru_W, gru_b, out):
         cod = {}
         scl = {}
         zt = {}
+        spare = {}
         at = {}
         bt_ = {}
         dts = {}
@@ -129,6 +135,7 @@ def tile_blockgrucell_pb_kernel(tc, y_dyn, deter, gru_W, gru_b, out):
                 stop=True,
             )
             zt[(h, tau, gate)] = z[:, half : half + 256]
+            spare[(h, tau, gate)] = z[:, 256 - half : 512 - half]
 
         def mx_ru(h):
             mx(h, 0, R, "zr")
@@ -165,16 +172,20 @@ def tile_blockgrucell_pb_kernel(tc, y_dyn, deter, gru_W, gru_b, out):
                 nc.scalar.activation(out=at[h][:, a:b], in_=at[h][:, a:b], func=ACT.Tanh)
 
         def p2(h):
-            tag, bufs = TAIL_D.get(h, ("dT", 1))
-            dts[h] = psum.tile([P, 2, 256], BF16, name="dT", tag=tag, bufs=bufs)
+            if h in D_BANK:
+                d = psum.tile([P, 256], F32, name="dT", tag=D_BANK[h], bufs=2)
+                dts[h] = d[:].bitcast(BF16)
+            else:
+                dts[h] = spare[(h + 1, 1, C)].bitcast(BF16)
             for tau in (0, 1):
                 for b in (0, 1):
                     n0 = P * (2 * (h % 4) + tau)
-                    nc.tensor.transpose(dts[h][:, tau, P * b : P * b + P], det[h // 4][:, b, n0 : n0 + P], ident_b[:])
+                    c0 = 256 * tau + P * b
+                    nc.tensor.transpose(dts[h][:, c0 : c0 + P], det[h // 4][:, b, n0 : n0 + P], ident_b[:])
 
         def v2(h):
             for a, b in pieces(h):
-                nc.vector.tensor_tensor(out=at[h][:, a:b], in0=at[h][:, a:b], in1=dts[h][:].rearrange("p t b -> p (t b)")[:, a:b], op=ALU.subtract)
+                nc.vector.tensor_tensor(out=at[h][:, a:b], in0=at[h][:, a:b], in1=dts[h][:, a:b], op=ALU.subtract)
 
         def v3(h):
             for a, b in pieces(h):
@@ -185,8 +196,7 @@ def tile_blockgrucell_pb_kernel(tc, y_dyn, deter, gru_W, gru_b, out):
             for i, (a, b) in enumerate(pieces(h)):
                 w = (b - a) // 2
                 n0 = 256 * (h % 4) + a // 2
-                tag, bufs = TAIL_E.get(h, (("eT", 1), ("dT", 1)))[i]
-                e = psum.tile([P, 2, w], F32, name="eT", tag=tag, bufs=bufs)
+                e = psum.tile([P, 2, w], F32, name="eT", tag=E_BANK.get(h, ("eT",))[i], bufs=2)
                 ets[h].append(e)
                 nc.tensor.matmul(out=e[:], lhsT=ident_b[:], rhs=det[h // 4][:, :, n0 : n0 + w], start=True, stop=False)
                 for s in range(w // P):
@@ -230,16 +240,9 @@ def tile_blockgrucell_pb_kernel(tc, y_dyn, deter, gru_W, gru_b, out):
         nc.vector.memset(brow[:], 0.0)
         nc.vector.memset(warm[:], 0.0)
         nc.sync.dma_start(out=brow[0:96, :], in_=gru_b.rearrange("(j p) -> j p", p=P))
-        load_chunk(1)
-        load_y(3)
-        load_y(6)
-        load_det(0)
-        load_y(1)
-        load_y(4)
-        load_chunk(2)
-        load_y(7)
-        load_chunk(3)
-        load_det(1)
+        LD = {"w": load_w, "c": load_chunk, "y": load_y, "d": load_det}
+        for kind, i in HEAD:
+            LD[kind](i)
         make_identity(nc, ident_f[:])
         make_identity(nc, ident_b[:])
         nc.scalar.activation(out=warm[:, 1:2], in_=warm[:, 0:1], func=ACT.Sigmoid)
@@ -260,7 +263,7 @@ def tile_blockgrucell_pb_kernel(tc, y_dyn, deter, gru_W, gru_b, out):
         yquant(5)
         y_turn(2, "zc", 2)
         y_copy(2)
-        bT = psum.tile([P, P], BF16, name="dT", tag="dT", bufs=1)
+        bT = psum.tile([P, P], BF16, name="bT", tag="eT", bufs=2)
         nc.tensor.transpose(bT[:], brow[:], ident_b[:])
         mx_ru(0)
         quantize(0, ((512, 768),))
@@ -269,24 +272,12 @@ def tile_blockgrucell_pb_kernel(tc, y_dyn, deter, gru_W, gru_b, out):
         yquant(2)
         quantize(1, ((512, 768),))
 
-        turn_a = {1: ((4, "eT"),)}
-        turn_b = {-1: ((3, "eT"), (6, "dT")), 0: ((1, "eT"),), 1: ((7, "eT"),)}
-        copy_a = {0: (3, 6), 1: (4,)}
-        copy_b = {0: (1,), 1: (7,)}
-        quant_q = {0: (3, 6), 1: (1,), 2: (7,)}
-        quant_e = {1: (4,)}
-        later = {0: (4,), 2: (5,), 4: (6,), 6: (7,)}
         for t in range(-1, NH + 3):
-            for j in later.get(t, ()):
-                load_chunk(j)
-            if t == 2:
-                load_det(2)
-                load_det(3)
-            for g, tag in turn_a.get(t, ()):
-                y_turn(g, tag, 1)
+            for kind, i in LATER.get(t, ()):
+                LD[kind](i)
             if 0 <= t + 1 < NH:
                 s1(t + 1)
-            for g in copy_a.get(t, ()):
+            for g in Y_COPY.get(t, ()):
                 y_copy(g)
             if 0 <= t - 2 < NH:
                 p3(t - 2)
@@ -294,33 +285,32 @@ def tile_blockgrucell_pb_kernel(tc, y_dyn, deter, gru_W, gru_b, out):
                 quantize(t + 2)
             if 0 <= t < NH:
                 v1(t)
-            if t < 2 and 0 <= t + 1 < NH:
+            if t < 2:
+                if t == 1:
+                    v2(0)
                 mx_c(t + 1)
             if 1 <= t + 2 < NH:
                 mx_ru(t + 2)
-            if 2 <= t < NH - 1:
-                mx_c(t + 1)
             if 2 <= t + 3 < NH:
                 il(t + 3, U, "s")
-            if 0 <= t - 2 < NH:
+            if 2 <= t < NH - 2:
                 v4(t - 2)
-            if 0 <= t - 1 < NH:
+            if 2 <= t < NH + 1:
                 v2(t - 1)
+            if 2 <= t < NH - 1:
+                mx_c(t + 1)
             if 0 <= t < NH:
                 p2(t)
-            if 0 <= t < NH:
                 s2(t)
             if 2 <= t + 3 < NH:
                 il(t + 3, R, "vgs")
                 il(t + 3, U, "vg")
                 il(t + 3, C, "vgs")
-            for g in quant_q.get(t, ()):
+            if NH - 2 <= t < NH + 2:
+                v4(t - 2)
+            for g in Y_QUANT.get(t, ()):
                 yquant(g)
-            for g, tag in turn_b.get(t, ()):
-                y_turn(g, tag, 1)
-            for g in copy_b.get(t, ()):
-                y_copy(g)
-            for g in quant_e.get(t, ()):
-                yquant(g)
+            for g in Y_TURN.get(t, ()):
+                y_turn(g, "eT", 2)
             if 0 <= t - 1 < NH:
                 v3(t - 1)

@@ -92,7 +92,7 @@ def tile_blockgrucell_pb_kernel(tc, y_dyn, deter, gru_W, gru_b, out):
             key = (h, gate == C)
             if key not in stg:
                 if gate == C:
-                    stg[key] = stgp.tile([P, 256, 4], BF16, name="stg_c", align_bytes=64, bufs=2)
+                    stg[key] = stgp.tile([P, 256, 4], BF16, name="stg_c", tag="stg_c0" if h == 0 else "stg_c", align_bytes=64, bufs=1)
                 else:
                     stg[key] = stgp.tile([P, 512, 4], BF16, name="stg_ru", align_bytes=64)
             st = stg[key]
@@ -281,8 +281,6 @@ def tile_blockgrucell_pb_kernel(tc, y_dyn, deter, gru_W, gru_b, out):
                 y_copy(g)
             if 0 <= t - 2 < NH:
                 p3(t - 2)
-            if 2 <= t + 2 < NH:
-                quantize(t + 2)
             if 0 <= t < NH:
                 v1(t)
             if t < 2:
@@ -303,14 +301,17 @@ def tile_blockgrucell_pb_kernel(tc, y_dyn, deter, gru_W, gru_b, out):
                 p2(t)
                 s2(t)
             if 2 <= t + 3 < NH:
-                il(t + 3, R, "vgs")
-                il(t + 3, U, "vg")
-                il(t + 3, C, "vgs")
+                for gate in (R, U, C) if t < 2 else (C, R, U):
+                    il(t + 3, gate, "vg" if gate == U else "vgs")
             if NH - 2 <= t < NH + 2:
                 v4(t - 2)
             for g in Y_QUANT.get(t, ()):
                 yquant(g)
             for g in Y_TURN.get(t, ()):
                 y_turn(g, "eT", 2)
+            if 2 <= t < NH - 3:
+                quantize(t + 3, ((512, 768),))
             if 0 <= t - 1 < NH:
                 v3(t - 1)
+            if t + 3 < NH:
+                quantize(t + 3, ((512, 768), (0, 512)) if t < 2 else ((0, 512),))

@@ -183,12 +183,15 @@ def tile_blockgrucell_pb_kernel(tc, y_dyn, deter, gru_W, gru_b, out):
                     c0 = 256 * tau + P * b
                     nc.tensor.transpose(dts[h][:, c0 : c0 + P], det[h // 4][:, b, n0 : n0 + P], ident_b[:])
 
+        def halves(h):
+            return ((0, 256), (256, 512)) if h in (12, 13, 14) else pieces(h)
+
         def v2(h):
-            for a, b in pieces(h):
+            for a, b in halves(h):
                 nc.vector.tensor_tensor(out=at[h][:, a:b], in0=at[h][:, a:b], in1=dts[h][:, a:b], op=ALU.subtract)
 
         def v3(h):
-            for a, b in pieces(h):
+            for a, b in halves(h):
                 nc.vector.tensor_tensor(out=at[h][:, a:b], in0=at[h][:, a:b], in1=bt_[h][:, a:b], op=ALU.mult)
 
         def p3(h):
@@ -266,8 +269,8 @@ def tile_blockgrucell_pb_kernel(tc, y_dyn, deter, gru_W, gru_b, out):
         bT = psum.tile([P, P], BF16, name="bT", tag="eT", bufs=2)
         nc.tensor.transpose(bT[:], brow[:], ident_b[:])
         mx_ru(0)
-        quantize(0, ((512, 768),))
         nc.vector.tensor_copy(out=bias[:], in_=bT[:])
+        quantize(0, ((512, 768),))
         nc.vector.tensor_scalar_add(out=bias[:, 64:96], in0=bias[:, 64:96], scalar1=-1.0)
         yquant(2)
         quantize(1, ((512, 768),))

from contextlib import ExitStack

import concourse.mybir as mybir
from concourse.masks import make_identity

F32 = mybir.dt.float32
BF16 = mybir.dt.bfloat16
U32 = mybir.dt.uint32
U8 = mybir.dt.uint8
E4 = mybir.dt.float8_e4m3fn_x4
E5 = mybir.dt.float8_e5m2_x4
ACT = mybir.ActivationFunctionType
ALU = mybir.AluOpType

FLOPS = 2 * 256 * 512 * 1536 * 8

P = 128
NH = 16
R, C, U = 0, 1, 2
YORD = (0, 5, 2, 3, 6, 1, 4, 7)
UNIT = {R: 0, U: 256, C: 512}
SHARES = ((2, ((160, 0), (160, 0), (160, 0))), (4, ((192, 0), (256, 0), (192, 0))), (5, ((256, 0), (256, 0), (0, 0))), (99, ((256, 0), (80, 176), (0, 0))),)

D_BANK = {13: "eT", 14: "zu", 15: "zu"}
E_BANK = {13: ("zr",), 15: ("eT", "zr")}
Y_TURN = {-1: (3, 6), 0: (1,), 2: (4,), 4: (7,)}
Y_COPY = {0: (3, 6), 1: (1,), 3: (4,), 5: (7,)}
Y_QUANT = {0: (3, 6), 2: (1,), 4: (4,), 6: (7,)}
HEAD = (("c", 1), ("y", 3), ("y", 6), ("d", 0), ("y", 1), ("c", 2), ("y", 4), ("y", 7), ("c", 3), ("d", 1))
LATER = {0: (("c", 4),), 2: (("c", 5), ("d", 2), ("d", 3)), 4: (("c", 6),), 6: (("c", 7),)}


def tile_blockgrucell_pb_kernel(tc, y_dyn, deter, gru_W, gru_b, out):
    nc = tc.nc
    y_v = y_dyn.rearrange("(bt p) d -> p bt d", p=P)
    det_v = deter.rearrange("(bt p) d -> p bt d", p=P)
    out_v = out.rearrange("(bt p) d -> p bt d", p=P)

    with ExitStack() as ctx:
        const = ctx.enter_context(tc.tile_pool(name="const", bufs=1))
        rawp = ctx.enter_context(tc.tile_pool(name="rawp", bufs=1))
        stgp = ctx.enter_context(tc.tile_pool(name="stgp", bufs=3))
        cdp = ctx.enter_context(tc.tile_pool(name="cdp", bufs=3))
        ygp = ctx.enter_context(tc.tile_pool(name="ygp", bufs=3))
        epp = ctx.enter_context(tc.tile_pool(name="epp", bufs=4))
        psum = ctx.enter_context(tc.psum_pool(name="psum", bufs=1))
        ctx.enter_context(tc.manual_schedule())

        ident_f = const.tile([P, P], F32, name="ident_f")
        ident_b = const.tile([P, P], BF16, name="ident_b")
        brow = const.tile([P, P], BF16, name="brow")
        bias = const.tile([P, P], F32, name="bias")
        warm = const.tile([P, 2], F32, name="warm")
        ycod = const.tile([P, 2048], U32, name="ycod", align_bytes=64)
        yscl = const.tile([P, 2048], U8, name="yscl", align_bytes=64)

        y_sb = {}
        det = {}
        raw = {}
        stg = {}
        cod = {}
        scl = {}
        zt = {}
        spare = {}
        at = {}
        bt_ = {}
        dts = {}
        ets = {}
        ygr = {}
        xts = {}

        def load_w(q):
            t = rawp.tile([P, 4, 512], BF16, name="w%d" % q)
            c0 = 512 * (q % 3)
            nc.sync.dma_start(out=t[:], in_=gru_W[q // 3, :, c0 : c0 + 512].rearrange("(p j) n -> p j n", j=4))
            raw[q] = t

        def load_chunk(j):
            load_w(j)
            load_w(16 + j)
            load_w(8 + j)

        def load_y(g):
            y_sb[g] = const.tile([P, 2, 512], BF16, name="y%d" % g)
            nc.sync.dma_start(out=y_sb[g][:], in_=y_v[:, :, 512 * g : 512 * g + 512])

        def load_det(k):
            det[k] = const.tile([P, 2, 1024], BF16, name="det%d" % k)
            nc.sync.dma_start(out=det[k][:], in_=det_v[:, :, 1024 * k : 1024 * k + 1024])

        def il(h, gate, eng="vgs"):
            key = (h, gate == C)
            if key not in stg:
                if gate == C:
                    stg[key] = stgp.tile([P, 256, 4], BF16, name="stg_c", tag="stg_c0" if h == 0 else "stg_c", align_bytes=64, bufs=1)
                else:
                    stg[key] = stgp.tile([P, 512, 4], BF16, name="stg_ru", align_bytes=64)
            st = stg[key]
            nv, ng = [sh for lim, sh in SHARES if h < lim][0][gate]
            c0 = 256 * (h % 2)
            u0 = UNIT[gate] % 512
            w = raw[8 * gate + h // 2]
            if nv > 0 and "v" in eng:
                nc.vector.tensor_copy(out=st[:, u0 : u0 + nv, :].rearrange("p (c i) j -> p c j i", i=8), in_=w[:, :, c0 : c0 + nv].rearrange("p j (c i) -> p c j i", i=8))
            if ng > 0 and "g" in eng:
                nc.gpsimd.tensor_scalar(out=st[:, u0 + nv : u0 + nv + ng, :], in0=w[:, :, c0 + nv : c0 + nv + ng].rearrange("p j w -> p w j"), scalar1=1.0, scalar2=0.0, op0=ALU.mult, op1=ALU.add)
            if nv + ng < 256 and "s" in eng:
                nc.scalar.copy(out=st[:, u0 + nv + ng : u0 + 256, :].rearrange("p (c i) j -> p c j i", i=8), in_=w[:, :, c0 + nv + ng : c0 + 256].rearrange("p j (c i) -> p c j i", i=8))

        def quantize(h, parts=((512, 768), (0, 512))):
            if h not in cod:
                cod[h] = cdp.tile([P, 768], U32, name="cod", align_bytes=64)
                scl[h] = cdp.tile([P, 768], U8, name="scl", align_bytes=64)
            for a, b in parts:
                nc.vector.quantize_mx(
                    out=cod[h][:, a:b].bitcast(E4),
                    scales=scl[h][:, a:b],
                    in_=stg[(h, a == 512)][:].rearrange("p w j -> p (w j)"),
                )

        def mx(h, tau, gate, tag):
            g = (8 * gate + h // 2) // 3
            pos = YORD.index(g)
            y0 = 256 * max(pos - 1, 0)
            half = 256 * pos - y0
            b0 = UNIT[gate] + P * tau
            z = psum.tile([P, 512], F32, name=tag, tag=tag, bufs=2)
            nc.tensor.matmul_mx(
                out=z[:],
                lhsT=cod[h][:, b0 : b0 + P].bitcast(E4),
                lhsT_scale=scl[h][:, b0 : b0 + P],
                rhs=ycod[:, y0 : y0 + 512].bitcast(E5),
                rhs_scale=yscl[:, y0 : y0 + 512],
                start=True,
                stop=True,
            )
            zt[(h, tau, gate)] = z[:, half : half + 256]
            spare[(h, tau, gate)] = z[:, 256 - half : 512 - half]

        def mx_ru(h):
            mx(h, 0, R, "zr")
            mx(h, 1, R, "zr")
            mx(h, 0, U, "zu")
            mx(h, 1, U, "zu")

        def mx_c(h):
            mx(h, 0, C, "zc")
            mx(h, 1, C, "zc")

        def bcol(h, tau, gate):
            j = 32 * gate + 2 * h + tau
            return bias[:, j : j + 1]

        def s1(h):
            at[h] = epp.tile([P, 512], F32, name="a_t")
            bt_[h] = epp.tile([P, 512], F32, name="b_t")
            for tau in (0, 1):
                nc.scalar.activation(out=at[h][:, 256 * tau : 256 * tau + 256], in_=zt[(h, tau, R)], func=ACT.Sigmoid, bias=bcol(h, tau, R), scale=1.0)
            for tau in (0, 1):
                nc.scalar.activation(out=bt_[h][:, 256 * tau : 256 * tau + 256], in_=zt[(h, tau, U)], func=ACT.Sigmoid, bias=bcol(h, tau, U), scale=1.0)

        def v1(h):
            for tau in (0, 1):
                sl = at[h][:, 256 * tau : 256 * tau + 256]
                nc.vector.scalar_tensor_tensor(out=sl, in0=zt[(h, tau, C)], scalar=bcol(h, tau, C), in1=sl, op0=ALU.add, op1=ALU.mult)

        def pieces(h):
            return ((0, 256), (256, 512)) if h == NH - 1 else ((0, 512),)

        def s2(h):
            for a, b in pieces(h):
                nc.scalar.activation(out=at[h][:, a:b], in_=at[h][:, a:b], func=ACT.Tanh)

        def p2(h):
            if h in D_BANK:
                d = psum.tile([P, 256], F32, name="dT", tag=D_BANK[h], bufs=2)
                dts[h] = d[:].bitcast(BF16)
            else:
                dts[h] = spare[(h + 1, 1, C)].bitcast(BF16)
            for tau in (0, 1):
                for b in (0, 1):
                    n0 = P * (2 * (h % 4) + tau)
                    c0 = 256 * tau + P * b
                    nc.tensor.transpose(dts[h][:, c0 : c0 + P], det[h // 4][:, b, n0 : n0 + P], ident_b[:])

        def halves(h):
            return ((0, 256), (256, 512)) if h in (12, 13, 14) else pieces(h)

        def v2(h):
            for a, b in halves(h):
                nc.vector.tensor_tensor(out=at[h][:, a:b], in0=at[h][:, a:b], in1=dts[h][:, a:b], op=ALU.subtract)

        def v3(h):
            for a, b in halves(h):
                nc.vector.tensor_tensor(out=at[h][:, a:b], in0=at[h][:, a:b], in1=bt_[h][:, a:b], op=ALU.mult)

        def p3(h):
            ets[h] = []
            for i, (a, b) in enumerate(pieces(h)):
                w = (b - a) // 2
                n0 = 256 * (h % 4) + a // 2
                e = psum.tile([P, 2, w], F32, name="eT", tag=E_BANK.get(h, ("eT",))[i], bufs=2)
                ets[h].append(e)
                nc.tensor.matmul(out=e[:], lhsT=ident_b[:], rhs=det[h // 4][:, :, n0 : n0 + w], start=True, stop=False)
                for s in range(w // P):
                    for bb in (0, 1):
                        c0 = a + 256 * s + P * bb
                        nc.tensor.matmul(out=e[:, bb, P * s : P * s + P], lhsT=at[h][:, c0 : c0 + P], rhs=ident_f[:], is_transpose=True, start=False, stop=(s == w // P - 1 and bb == 1))

        def v4(h):
            for i, (a, b) in enumerate(pieces(h)):
                w = (b - a) // 2
                o = epp.tile([P, 2, w], F32, name="o_t", bufs=8)
                nc.scalar.copy(out=o[:], in_=ets[h][i][:])
                nc.sync.dma_start(out=out_v[:, :, 256 * h + a // 2 : 256 * h + a // 2 + w], in_=o[:])

        def y_turn(g, tag, bufs):
            xt = psum.tile([P, 2, 256], F32, name=tag, tag=tag, bufs=bufs)
            xts[g] = xt
            for b in (0, 1):
                words = y_sb[g][:, b, :].bitcast(F32)
                for u in (0, 1):
                    nc.tensor.transpose(xt[:, u, P * b : P * b + P], words[:, u : 256 : 2], ident_f[:])

        def y_copy(g):
            ygr[g] = ygp.tile([P, 256, 4], BF16, name="ygr", align_bytes=64)
            nc.scalar.copy(out=ygr[g][:].bitcast(F32), in_=xts[g][:].rearrange("p u b -> p b u"))

        def yquant(g):
            c0 = 256 * YORD.index(g)
            nc.vector.quantize_mx(
                out=ycod[:, c0 : c0 + 256].bitcast(E5),
                scales=yscl[:, c0 : c0 + 256],
                in_=ygr[g][:].rearrange("p w j -> p (w j)"),
            )

        load_w(0)
        load_y(0)
        load_w(16)
        load_y(5)
        load_w(8)
        load_y(2)
        nc.vector.memset(brow[:], 0.0)
        nc.vector.memset(warm[:], 0.0)
        nc.sync.dma_start(out=brow[0:96, :], in_=gru_b.rearrange("(j p) -> j p", p=P))
        LD = {"w": load_w, "c": load_chunk, "y": load_y, "d": load_det}
        for kind, i in HEAD:
            LD[kind](i)
        make_identity(nc, ident_f[:])
        make_identity(nc, ident_b[:])
        nc.scalar.activation(out=warm[:, 1:2], in_=warm[:, 0:1], func=ACT.Sigmoid)

        il(0, R)
        il(1, R)
        y_turn(0, "zr", 2)
        y_copy(0)
        il(0, U)
        il(1, U)
        y_turn(5, "zu", 2)
        y_copy(5)
        quantize(0, ((0, 512),))
        yquant(0)
        quantize(1, ((0, 512),))
        il(0, C)
        il(1, C)
        yquant(5)
        y_turn(2, "zc", 2)
        y_copy(2)
        bT = psum.tile([P, P], BF16, name="bT", tag="eT", bufs=2)
        nc.tensor.transpose(bT[:], brow[:], ident_b[:])
        mx_ru(0)
        nc.vector.tensor_copy(out=bias[:], in_=bT[:])
        quantize(0, ((512, 768),))
        nc.vector.tensor_scalar_add(out=bias[:, 64:96], in0=bias[:, 64:96], scalar1=-1.0)
        yquant(2)
        quantize(1, ((512, 768),))

        for t in range(-1, NH + 3):
            for kind, i in LATER.get(t, ()):
                LD[kind](i)
            if 0 <= t + 1 < NH:
                s1(t + 1)
            for g in Y_COPY.get(t, ()):
                y_copy(g)
            if 0 <= t - 2 < NH:
                p3(t - 2)
            if 0 <= t < NH:
                v1(t)
            if t < 2:
                if t == 1:
                    v2(0)
                mx_c(t + 1)
            if 1 <= t + 2 < NH:
                mx_ru(t + 2)
            if 2 <= t + 3 < NH:
                il(t + 3, U, "s")
            if 2 <= t < NH - 2:
                v4(t - 2)
            if 2 <= t < NH + 1:
                v2(t - 1)
            if 2 <= t < NH - 1:
                mx_c(t + 1)
            if 0 <= t < NH:
                p2(t)
                s2(t)
            if 2 <= t + 3 < NH:
                for gate in (R, U, C) if t < 2 else (C, R, U):
                    il(t + 3, gate, "vg" if gate == U else "vgs")
            if NH - 2 <= t < NH + 2:
                v4(t - 2)
            for g in Y_QUANT.get(t, ()):
                yquant(g)
            for g in Y_TURN.get(t, ()):
                y_turn(g, "eT", 2)
            if 2 <= t < NH - 3:
                quantize(t + 3, ((512, 768),))
            if 0 <= t - 1 < NH:
                v3(t - 1)
            if t + 3 < NH:
                quantize(t + 3, ((512, 768), (0, 512)) if t < 2 else ((0, 512),))
